import numpy as np
import ml_dtypes

BF16 = ml_dtypes.bfloat16


def bf(x):
    return np.asarray(x, np.float32).astype(BF16)


def f32(x):
    return np.asarray(x, np.float32)


def f64(x):
    return np.asarray(x).astype(np.float64)


def striped(idx):
    return np.tile(idx.reshape(-1, 16).T, (8, 1))


E1, E2, S, N, H = 128, 128, 1024, 1024, 128
ALPHA = 0.25


def setup_inputs():
    return {
        "query": f32(np.random.standard_normal((E2, S))),
        "x": f32(np.random.standard_normal((E1, N))),
        "wx": bf(0.5 * np.random.standard_normal((E1, H)) / np.sqrt(E1)),
        "wp": bf(np.random.standard_normal((E1 * E2, H)) / np.sqrt(E1 * E2)),
        "b1": f32(0.1 * np.random.standard_normal((H, 1))),
        "offs": striped(np.random.permutation(np.tile(np.arange(S), 2))[:N]),
    }


def reference(query, x, wx, wp, b1, offs):
    idx = offs[:16].T.reshape(-1)
    q = f64(query)[:, idx]
    xx = f64(x)
    p = (xx[:, None, :] * q[None, :, :]).reshape(E1 * E2, N)
    u = f64(wx).T @ xx + f64(wp).T @ p + f64(b1)
    avg = u.mean(axis=1, keepdims=True)
    std = np.sqrt(((u - avg) ** 2).sum(axis=1, keepdims=True) / (N - 1))
    s = 1.0 / (1.0 + np.exp(-(u - avg) / std))
    return u * s + ALPHA * u * (1.0 - s)

@@ -1,0 +1,97 @@
+import concourse.mybir as mybir
+
+F32, BF16, U16 = mybir.dt.float32, mybir.dt.bfloat16, mybir.dt.uint16
+MULT, ADD, POW = mybir.AluOpType.mult, mybir.AluOpType.add, mybir.AluOpType.pow
+IDENTITY = mybir.ActivationFunctionType.Identity
+SIGMOID = mybir.ActivationFunctionType.Sigmoid
+
+P = 128
+N = 1024
+BANK = 512
+HALVES = N // BANK
+BLOCKS_PER_LOAD = 16
+ALPHA = 0.25
+
+FLOPS = 2 * (P * P + P) * P * N
+
+
+def tile_attention_kernel(tc, query, x, wx, wp, b1, offs, out):
+    nc = tc.nc
+    with (
+        tc.tile_pool(name="lists", bufs=1) as lists,
+        tc.tile_pool(name="held", bufs=1) as held,
+        tc.tile_pool(name="spread", bufs=4) as spread,
+        tc.tile_pool(name="products", bufs=3) as products,
+        tc.psum_pool(name="psum", bufs=1) as psum,
+    ):
+        offsets = lists.tile([P, N // 16], U16, name="offsets")
+        nc.sync.dma_start(offsets[:], offs)
+        window = held.tile([P, N], F32, name="window")
+        nc.sync.dma_start(window[:], query)
+
+        x_f32 = held.tile([P, N], F32, name="x_f32")
+        nc.scalar.dma_start(x_f32[:], x)
+        wx_tile = held.tile([P, P], BF16, name="wx_tile")
+        nc.scalar.dma_start(wx_tile[:], wx)
+        bias = held.tile([P, 1], F32, name="bias")
+        nc.scalar.dma_start(bias[:], b1)
+        minus_half = held.tile([P, 1], F32, name="minus_half")
+        nc.gpsimd.memset(minus_half[:], -0.5)
+
+        wp_blocks = wp.rearrange("(i e) m -> e i m", e=P)
+        wp_tiles = []
+
+        def load_wp_tile():
+            first = len(wp_tiles) * BLOCKS_PER_LOAD
+            wp_tile = held.tile([P, BLOCKS_PER_LOAD, P], BF16, name=f"wp_tile{first}")
+            nc.scalar.dma_start(wp_tile[:], wp_blocks[:, first : first + BLOCKS_PER_LOAD, :])
+            wp_tiles.append(wp_tile)
+
+        load_wp_tile()
+
+        u_psum = [psum.tile([P, BANK], F32, name=f"u_psum{h}") for h in range(HALVES)]
+
+        x_bf16 = held.tile([P, N], BF16, name="x_bf16")
+        nc.scalar.copy(x_bf16[:], x_f32[:])
+        for h in range(HALVES):
+            nc.tensor.matmul(u_psum[h][:], wx_tile[:], x_bf16[:, h * BANK : (h + 1) * BANK], start=True, stop=False)
+
+        for i in range(P):
+            if i % BLOCKS_PER_LOAD == 0 and i + BLOCKS_PER_LOAD < P:
+                load_wp_tile()
+            x_row = spread.tile([P, N], F32, name="x_row")
+            nc.sync.dma_start(x_row[:], x[i, :].partition_broadcast(P))
+            product_f32 = products.tile([P, N], F32, name="product_f32")
+            nc.vector.tensor_tensor(product_f32[:], window[:].indirect(offsets[:]), x_row[:], MULT)
+            product = products.tile([P, N], BF16, name="product")
+            nc.scalar.copy(product[:], product_f32[:])
+            weights = wp_tiles[i // BLOCKS_PER_LOAD][:, i % BLOCKS_PER_LOAD, :]
+            for h in range(HALVES):
+                nc.tensor.matmul(
+                    u_psum[h][:], weights, product[:, h * BANK : (h + 1) * BANK], start=False, stop=(i == P - 1)
+                )
+
+        u = held.tile([P, N], F32, name="u")
+        stats = held.tile([P, HALVES * 6], F32, name="stats")
+        for h in range(HALVES):
+            half = slice(h * BANK, (h + 1) * BANK)
+            nc.scalar.activation(u[:, half], u_psum[h][:], IDENTITY, bias=bias[:, 0:1])
+            nc.vector.bn_stats(stats[:, h * 6 : (h + 1) * 6], u[:, half])
+        mean_var = held.tile([P, 2], F32, name="mean_var")
+        nc.vector.bn_aggr(mean_var[:], stats[:])
+
+        inv_root = held.tile([P, 1], F32, name="inv_root")
+        nc.gpsimd.tensor_tensor(inv_root[:], mean_var[:, 1:2], minus_half[:], POW)
+        inv_std = held.tile([P, 1], F32, name="inv_std")
+        nc.gpsimd.tensor_scalar(inv_std[:], inv_root[:], ((N - 1) / N) ** 0.5, None, MULT)
+        shift = held.tile([P, 1], F32, name="shift")
+        nc.gpsimd.tensor_scalar(shift[:], mean_var[:, 0:1], inv_std[:, 0:1], -1.0, MULT, MULT)
+
+        gate = held.tile([P, N], F32, name="gate")
+        result = held.tile([P, N], F32, name="result")
+        for h in range(HALVES):
+            half = slice(h * BANK, (h + 1) * BANK)
+            nc.scalar.activation(gate[:, half], u[:, half], SIGMOID, bias=shift[:, 0:1], scale=inv_std[:, 0:1])
+            nc.vector.tensor_scalar(gate[:, half], gate[:, half], 1.0 - ALPHA, ALPHA, MULT, ADD)
+            nc.vector.tensor_tensor(result[:, half], gate[:, half], u[:, half], MULT)
+            nc.sync.dma_start(out[:, half], result[:, half])

@@ -11,6 +11,7 @@ BANK = 512
 HALVES = N // BANK
 BLOCKS_PER_LOAD = 16
 ALPHA = 0.25
+UNBIAS = ((N - 1) / N) ** 0.5
 
 FLOPS = 2 * (P * P + P) * P * N
 
@@ -37,6 +38,8 @@ def tile_attention_kernel(tc, query, x, wx, wp, b1, offs, out):
         nc.scalar.dma_start(bias[:], b1)
         minus_half = held.tile([P, 1], F32, name="minus_half")
         nc.gpsimd.memset(minus_half[:], -0.5)
+        warm = held.tile([P, 1], F32, name="warm")
+        nc.scalar.activation(warm[:], minus_half[:], SIGMOID)
 
         wp_blocks = wp.rearrange("(i e) m -> e i m", e=P)
         wp_tiles = []
@@ -64,34 +67,33 @@ def tile_attention_kernel(tc, query, x, wx, wp, b1, offs, out):
             product_f32 = products.tile([P, N], F32, name="product_f32")
             nc.vector.tensor_tensor(product_f32[:], window[:].indirect(offsets[:]), x_row[:], MULT)
             product = products.tile([P, N], BF16, name="product")
-            nc.scalar.copy(product[:], product_f32[:])
             weights = wp_tiles[i // BLOCKS_PER_LOAD][:, i % BLOCKS_PER_LOAD, :]
             for h in range(HALVES):
-                nc.tensor.matmul(
-                    u_psum[h][:], weights, product[:, h * BANK : (h + 1) * BANK], start=False, stop=(i == P - 1)
-                )
+                half = slice(h * BANK, (h + 1) * BANK)
+                nc.scalar.copy(product[:, half], product_f32[:, half])
+                nc.tensor.matmul(u_psum[h][:], weights, product[:, half], start=False, stop=(i == P - 1))
 
         u = held.tile([P, N], F32, name="u")
         stats = held.tile([P, HALVES * 6], F32, name="stats")
         for h in range(HALVES):
-            half = slice(h * BANK, (h + 1) * BANK)
-            nc.scalar.activation(u[:, half], u_psum[h][:], IDENTITY, bias=bias[:, 0:1])
-            nc.vector.bn_stats(stats[:, h * 6 : (h + 1) * 6], u[:, half])
+            other = HALVES - 1 - h
+            nc.vector.bn_stats(stats[:, h * 6 : (h + 1) * 6], u_psum[h][:])
+            nc.scalar.activation(u[:, other * BANK : (other + 1) * BANK], u_psum[other][:], IDENTITY, bias=bias[:, 0:1])
         mean_var = held.tile([P, 2], F32, name="mean_var")
         nc.vector.bn_aggr(mean_var[:], stats[:])
 
         inv_root = held.tile([P, 1], F32, name="inv_root")
         nc.gpsimd.tensor_tensor(inv_root[:], mean_var[:, 1:2], minus_half[:], POW)
         inv_std = held.tile([P, 1], F32, name="inv_std")
-        nc.gpsimd.tensor_scalar(inv_std[:], inv_root[:], ((N - 1) / N) ** 0.5, None, MULT)
+        nc.gpsimd.tensor_scalar(inv_std[:], inv_root[:], UNBIAS, None, MULT)
         shift = held.tile([P, 1], F32, name="shift")
-        nc.gpsimd.tensor_scalar(shift[:], mean_var[:, 0:1], inv_std[:, 0:1], -1.0, MULT, MULT)
+        nc.vector.tensor_scalar(shift[:], mean_var[:, 0:1], inv_root[:, 0:1], -UNBIAS, MULT, MULT)
 
         gate = held.tile([P, N], F32, name="gate")
         result = held.tile([P, N], F32, name="result")
         for h in range(HALVES):
             half = slice(h * BANK, (h + 1) * BANK)
-            nc.scalar.activation(gate[:, half], u[:, half], SIGMOID, bias=shift[:, 0:1], scale=inv_std[:, 0:1])
+            nc.scalar.activation(gate[:, half], u_psum[h][:], SIGMOID, bias=shift[:, 0:1], scale=inv_std[:, 0:1])
             nc.vector.tensor_scalar(gate[:, half], gate[:, half], 1.0 - ALPHA, ALPHA, MULT, ADD)
             nc.vector.tensor_tensor(result[:, half], gate[:, half], u[:, half], MULT)
             nc.sync.dma_start(out[:, half], result[:, half])

@@ -9,7 +9,8 @@ P = 128
 N = 1024
 BANK = 512
 HALVES = N // BANK
-BLOCKS_PER_LOAD = 16
+GROUP = 16
+GROUPS = P // GROUP
 ALPHA = 0.25
 UNBIAS = ((N - 1) / N) ** 0.5
 
@@ -21,14 +22,33 @@ def tile_attention_kernel(tc, query, x, wx, wp, b1, offs, out):
     with (
         tc.tile_pool(name="lists", bufs=1) as lists,
         tc.tile_pool(name="held", bufs=1) as held,
-        tc.tile_pool(name="spread", bufs=4) as spread,
         tc.tile_pool(name="products", bufs=3) as products,
         tc.psum_pool(name="psum", bufs=1) as psum,
     ):
         offsets = lists.tile([P, N // 16], U16, name="offsets")
         nc.sync.dma_start(offsets[:], offs)
-        window = held.tile([P, N], F32, name="window")
-        nc.sync.dma_start(window[:], query)
+
+        def load_window(a):
+            window = held.tile([P, N], F32, name=f"window{a}")
+            for h in range(GROUPS):
+                nc.sync.dma_start(
+                    window[h * GROUP : (h + 1) * GROUP, :], query[h * GROUP + a, :].partition_broadcast(GROUP)
+                )
+            return window
+
+        def load_x_rows(c):
+            x_rows = held.tile([P, N], F32, name=f"x_rows{c}")
+            for h in range(GROUPS):
+                nc.sync.dma_start(x_rows[h * GROUP : (h + 1) * GROUP, :], x[c * GROUP : (c + 1) * GROUP, :])
+            return x_rows
+
+        wp_runs = wp.rearrange("(c l h a) m -> c h l (a m)", c=GROUPS, l=GROUP, h=GROUPS, a=GROUP)
+
+        def load_wp_blocks(c):
+            wp_blocks = held.tile([P, GROUP * P], BF16, name=f"wp_blocks{c}")
+            for h in range(GROUPS):
+                nc.sync.dma_start(wp_blocks[h * GROUP : (h + 1) * GROUP, :], wp_runs[c, h])
+            return wp_blocks
 
         x_f32 = held.tile([P, N], F32, name="x_f32")
         nc.scalar.dma_start(x_f32[:], x)
@@ -41,17 +61,6 @@ def tile_attention_kernel(tc, query, x, wx, wp, b1, offs, out):
         warm = held.tile([P, 1], F32, name="warm")
         nc.scalar.activation(warm[:], minus_half[:], SIGMOID)
 
-        wp_blocks = wp.rearrange("(i e) m -> e i m", e=P)
-        wp_tiles = []
-
-        def load_wp_tile():
-            first = len(wp_tiles) * BLOCKS_PER_LOAD
-            wp_tile = held.tile([P, BLOCKS_PER_LOAD, P], BF16, name=f"wp_tile{first}")
-            nc.scalar.dma_start(wp_tile[:], wp_blocks[:, first : first + BLOCKS_PER_LOAD, :])
-            wp_tiles.append(wp_tile)
-
-        load_wp_tile()
-
         u_psum = [psum.tile([P, BANK], F32, name=f"u_psum{h}") for h in range(HALVES)]
 
         x_bf16 = held.tile([P, N], BF16, name="x_bf16")
@@ -59,19 +68,23 @@ def tile_attention_kernel(tc, query, x, wx, wp, b1, offs, out):
         for h in range(HALVES):
             nc.tensor.matmul(u_psum[h][:], wx_tile[:], x_bf16[:, h * BANK : (h + 1) * BANK], start=True, stop=False)
 
-        for i in range(P):
-            if i % BLOCKS_PER_LOAD == 0 and i + BLOCKS_PER_LOAD < P:
-                load_wp_tile()
-            x_row = spread.tile([P, N], F32, name="x_row")
-            nc.sync.dma_start(x_row[:], x[i, :].partition_broadcast(P))
-            product_f32 = products.tile([P, N], F32, name="product_f32")
-            nc.vector.tensor_tensor(product_f32[:], window[:].indirect(offsets[:]), x_row[:], MULT)
-            product = products.tile([P, N], BF16, name="product")
-            weights = wp_tiles[i // BLOCKS_PER_LOAD][:, i % BLOCKS_PER_LOAD, :]
-            for h in range(HALVES):
-                half = slice(h * BANK, (h + 1) * BANK)
-                nc.scalar.copy(product[:, half], product_f32[:, half])
-                nc.tensor.matmul(u_psum[h][:], weights, product[:, half], start=False, stop=(i == P - 1))
+        windows = []
+        for c in range(GROUPS):
+            x_rows = load_x_rows(c)
+            wp_blocks = load_wp_blocks(c)
+            for a in range(GROUP):
+                if c == 0:
+                    windows.append(load_window(a))
+                product_f32 = products.tile([P, N], F32, name="product_f32")
+                nc.vector.tensor_tensor(product_f32[:], windows[a][:].indirect(offsets[:]), x_rows[:], MULT)
+                product = products.tile([P, N], BF16, name="product")
+                last = c == GROUPS - 1 and a == GROUP - 1
+                for h in range(HALVES):
+                    half = slice(h * BANK, (h + 1) * BANK)
+                    nc.scalar.copy(product[:, half], product_f32[:, half])
+                    nc.tensor.matmul(
+                        u_psum[h][:], wp_blocks[:, a * P : (a + 1) * P], product[:, half], start=False, stop=last
+                    )
 
         u = held.tile([P, N], F32, name="u")
         stats = held.tile([P, HALVES * 6], F32, name="stats")

@@ -9,8 +9,7 @@ P = 128
 N = 1024
 BANK = 512
 HALVES = N // BANK
-GROUP = 16
-GROUPS = P // GROUP
+CHUNK = 16
 ALPHA = 0.25
 UNBIAS = ((N - 1) / N) ** 0.5
 
@@ -22,33 +21,12 @@ def tile_attention_kernel(tc, query, x, wx, wp, b1, offs, out):
     with (
         tc.tile_pool(name="lists", bufs=1) as lists,
         tc.tile_pool(name="held", bufs=1) as held,
+        tc.tile_pool(name="windows", bufs=4) as windows,
         tc.tile_pool(name="products", bufs=3) as products,
         tc.psum_pool(name="psum", bufs=1) as psum,
     ):
         offsets = lists.tile([P, N // 16], U16, name="offsets")
         nc.sync.dma_start(offsets[:], offs)
-
-        def load_window(a):
-            window = held.tile([P, N], F32, name=f"window{a}")
-            for h in range(GROUPS):
-                nc.sync.dma_start(
-                    window[h * GROUP : (h + 1) * GROUP, :], query[h * GROUP + a, :].partition_broadcast(GROUP)
-                )
-            return window
-
-        def load_x_rows(c):
-            x_rows = held.tile([P, N], F32, name=f"x_rows{c}")
-            for h in range(GROUPS):
-                nc.sync.dma_start(x_rows[h * GROUP : (h + 1) * GROUP, :], x[c * GROUP : (c + 1) * GROUP, :])
-            return x_rows
-
-        wp_runs = wp.rearrange("(c l h a) m -> c h l (a m)", c=GROUPS, l=GROUP, h=GROUPS, a=GROUP)
-
-        def load_wp_blocks(c):
-            wp_blocks = held.tile([P, GROUP * P], BF16, name=f"wp_blocks{c}")
-            for h in range(GROUPS):
-                nc.sync.dma_start(wp_blocks[h * GROUP : (h + 1) * GROUP, :], wp_runs[c, h])
-            return wp_blocks
 
         x_f32 = held.tile([P, N], F32, name="x_f32")
         nc.scalar.dma_start(x_f32[:], x)
@@ -61,30 +39,31 @@ def tile_attention_kernel(tc, query, x, wx, wp, b1, offs, out):
         warm = held.tile([P, 1], F32, name="warm")
         nc.scalar.activation(warm[:], minus_half[:], SIGMOID)
 
+        wp_rows = wp.rearrange("(i e) m -> i (e m)", i=P)
+
         u_psum = [psum.tile([P, BANK], F32, name=f"u_psum{h}") for h in range(HALVES)]
 
-        x_bf16 = held.tile([P, N], BF16, name="x_bf16")
-        nc.scalar.copy(x_bf16[:], x_f32[:])
-        for h in range(HALVES):
-            nc.tensor.matmul(u_psum[h][:], wx_tile[:], x_bf16[:, h * BANK : (h + 1) * BANK], start=True, stop=False)
-
-        windows = []
-        for c in range(GROUPS):
-            x_rows = load_x_rows(c)
-            wp_blocks = load_wp_blocks(c)
-            for a in range(GROUP):
-                if c == 0:
-                    windows.append(load_window(a))
-                product_f32 = products.tile([P, N], F32, name="product_f32")
-                nc.vector.tensor_tensor(product_f32[:], windows[a][:].indirect(offsets[:]), x_rows[:], MULT)
-                product = products.tile([P, N], BF16, name="product")
-                last = c == GROUPS - 1 and a == GROUP - 1
+        for e in range(P):
+            window = windows.tile([P, N], F32, name="window")
+            nc.sync.dma_start(window[:], query[e, :].partition_broadcast(P))
+            if e % CHUNK == 0:
+                wp_blocks = held.tile([P, CHUNK * P], BF16, name=f"wp_blocks{e // CHUNK}")
+                nc.sync.dma_start(wp_blocks[:], wp_rows[:, e * P : (e + CHUNK) * P])
+            if e == 0:
+                x_bf16 = held.tile([P, N], BF16, name="x_bf16")
+                nc.scalar.copy(x_bf16[:], x_f32[:])
                 for h in range(HALVES):
-                    half = slice(h * BANK, (h + 1) * BANK)
-                    nc.scalar.copy(product[:, half], product_f32[:, half])
                     nc.tensor.matmul(
-                        u_psum[h][:], wp_blocks[:, a * P : (a + 1) * P], product[:, half], start=False, stop=last
+                        u_psum[h][:], wx_tile[:], x_bf16[:, h * BANK : (h + 1) * BANK], start=True, stop=False
                     )
+            product_f32 = products.tile([P, N], F32, name="product_f32")
+            nc.vector.tensor_tensor(product_f32[:], window[:].indirect(offsets[:]), x_f32[:], MULT)
+            product = products.tile([P, N], BF16, name="product")
+            block = slice((e % CHUNK) * P, (e % CHUNK + 1) * P)
+            for h in range(HALVES):
+                half = slice(h * BANK, (h + 1) * BANK)
+                nc.scalar.copy(product[:, half], product_f32[:, half])
+                nc.tensor.matmul(u_psum[h][:], wp_blocks[:, block], product[:, half], start=False, stop=e == P - 1)
 
         u = held.tile([P, N], F32, name="u")
         stats = held.tile([P, HALVES * 6], F32, name="stats")

@@ -34,6 +34,8 @@ def tile_attention_kernel(tc, query, x, wx, wp, b1, offs, out):
         nc.scalar.dma_start(wx_tile[:], wx)
         bias = held.tile([P, 1], F32, name="bias")
         nc.scalar.dma_start(bias[:], b1)
+        scaled_bias = held.tile([P, 1], F32, name="scaled_bias")
+        nc.gpsimd.tensor_scalar(scaled_bias[:], bias[:], 1.0 - ALPHA, None, MULT)
         minus_half = held.tile([P, 1], F32, name="minus_half")
         nc.gpsimd.memset(minus_half[:], -0.5)
         warm = held.tile([P, 1], F32, name="warm")
@@ -57,7 +59,14 @@ def tile_attention_kernel(tc, query, x, wx, wp, b1, offs, out):
                         u_psum[h][:], wx_tile[:], x_bf16[:, h * BANK : (h + 1) * BANK], start=True, stop=False
                     )
             product_f32 = products.tile([P, N], F32, name="product_f32")
-            nc.vector.tensor_tensor(product_f32[:], window[:].indirect(offsets[:]), x_f32[:], MULT)
+            piece = BANK if e == P - 1 else N
+            for first in range(0, N, piece):
+                nc.vector.tensor_tensor(
+                    product_f32[:, first : first + piece],
+                    window[:].indirect(offsets[:, first // 16 : (first + piece) // 16]),
+                    x_f32[:, first : first + piece],
+                    MULT,
+                )
             product = products.tile([P, N], BF16, name="product")
             block = slice((e % CHUNK) * P, (e % CHUNK + 1) * P)
             for h in range(HALVES):
@@ -65,19 +74,21 @@ def tile_attention_kernel(tc, query, x, wx, wp, b1, offs, out):
                 nc.scalar.copy(product[:, half], product_f32[:, half])
                 nc.tensor.matmul(u_psum[h][:], wp_blocks[:, block], product[:, half], start=False, stop=e == P - 1)
 
-        u = held.tile([P, N], F32, name="u")
         stats = held.tile([P, HALVES * 6], F32, name="stats")
         for h in range(HALVES):
-            other = HALVES - 1 - h
             nc.vector.bn_stats(stats[:, h * 6 : (h + 1) * 6], u_psum[h][:])
-            nc.scalar.activation(u[:, other * BANK : (other + 1) * BANK], u_psum[other][:], IDENTITY, bias=bias[:, 0:1])
         mean_var = held.tile([P, 2], F32, name="mean_var")
         nc.vector.bn_aggr(mean_var[:], stats[:])
+
+        scaled_u = held.tile([P, N], F32, name="scaled_u")
+        for h in range(HALVES):
+            half = slice(h * BANK, (h + 1) * BANK)
+            nc.scalar.activation(scaled_u[:, half], u_psum[h][:], IDENTITY, bias=scaled_bias[:, 0:1], scale=1.0 - ALPHA)
 
         inv_root = held.tile([P, 1], F32, name="inv_root")
         nc.gpsimd.tensor_tensor(inv_root[:], mean_var[:, 1:2], minus_half[:], POW)
         inv_std = held.tile([P, 1], F32, name="inv_std")
-        nc.gpsimd.tensor_scalar(inv_std[:], inv_root[:], UNBIAS, None, MULT)
+        nc.vector.tensor_scalar(inv_std[:], inv_root[:], UNBIAS, None, MULT)
         shift = held.tile([P, 1], F32, name="shift")
         nc.vector.tensor_scalar(shift[:], mean_var[:, 0:1], inv_root[:, 0:1], -UNBIAS, MULT, MULT)
 
@@ -86,6 +97,7 @@ def tile_attention_kernel(tc, query, x, wx, wp, b1, offs, out):
         for h in range(HALVES):
             half = slice(h * BANK, (h + 1) * BANK)
             nc.scalar.activation(gate[:, half], u_psum[h][:], SIGMOID, bias=shift[:, 0:1], scale=inv_std[:, 0:1])
-            nc.vector.tensor_scalar(gate[:, half], gate[:, half], 1.0 - ALPHA, ALPHA, MULT, ADD)
-            nc.vector.tensor_tensor(result[:, half], gate[:, half], u[:, half], MULT)
+            nc.vector.scalar_tensor_tensor(
+                result[:, half], gate[:, half], ALPHA / (1.0 - ALPHA), scaled_u[:, half], ADD, MULT
+            )
             nc.sync.dma_start(out[:, half], result[:, half])

@@ -68,10 +68,11 @@ def tile_attention_kernel(tc, query, x, wx, wp, b1, offs, out):
                     MULT,
                 )
             product = products.tile([P, N], BF16, name="product")
+            for first in range(0, N, piece):
+                nc.scalar.copy(product[:, first : first + piece], product_f32[:, first : first + piece])
             block = slice((e % CHUNK) * P, (e % CHUNK + 1) * P)
             for h in range(HALVES):
                 half = slice(h * BANK, (h + 1) * BANK)
-                nc.scalar.copy(product[:, half], product_f32[:, half])
                 nc.tensor.matmul(u_psum[h][:], wp_blocks[:, block], product[:, half], start=False, stop=e == P - 1)
 
         stats = held.tile([P, HALVES * 6], F32, name="stats")

@@ -21,7 +21,7 @@ def tile_attention_kernel(tc, query, x, wx, wp, b1, offs, out):
     with (
         tc.tile_pool(name="lists", bufs=1) as lists,
         tc.tile_pool(name="held", bufs=1) as held,
-        tc.tile_pool(name="windows", bufs=4) as windows,
+        tc.tile_pool(name="windows", bufs=8) as windows,
         tc.tile_pool(name="products", bufs=3) as products,
         tc.psum_pool(name="psum", bufs=1) as psum,
     ):

@@ -10,6 +10,7 @@ N = 1024
 BANK = 512
 HALVES = N // BANK
 CHUNK = 16
+LAST_PIECE = 256
 ALPHA = 0.25
 UNBIAS = ((N - 1) / N) ** 0.5
 
@@ -59,7 +60,7 @@ def tile_attention_kernel(tc, query, x, wx, wp, b1, offs, out):
                         u_psum[h][:], wx_tile[:], x_bf16[:, h * BANK : (h + 1) * BANK], start=True, stop=False
                     )
             product_f32 = products.tile([P, N], F32, name="product_f32")
-            piece = BANK if e == P - 1 else N
+            piece = LAST_PIECE if e == P - 1 else N
             for first in range(0, N, piece):
                 nc.vector.tensor_tensor(
                     product_f32[:, first : first + piece],
@@ -69,11 +70,21 @@ def tile_attention_kernel(tc, query, x, wx, wp, b1, offs, out):
                 )
             product = products.tile([P, N], BF16, name="product")
             for first in range(0, N, piece):
-                nc.scalar.copy(product[:, first : first + piece], product_f32[:, first : first + piece])
+                if e == P - 1 and first + piece == N:
+                    nc.vector.tensor_copy(product[:, first : first + piece], product_f32[:, first : first + piece])
+                else:
+                    nc.scalar.copy(product[:, first : first + piece], product_f32[:, first : first + piece])
             block = slice((e % CHUNK) * P, (e % CHUNK + 1) * P)
-            for h in range(HALVES):
-                half = slice(h * BANK, (h + 1) * BANK)
-                nc.tensor.matmul(u_psum[h][:], wp_blocks[:, block], product[:, half], start=False, stop=e == P - 1)
+            width = min(piece, BANK)
+            for first in range(0, N, width):
+                h, column = first // BANK, first % BANK
+                nc.tensor.matmul(
+                    u_psum[h][:, column : column + width],
+                    wp_blocks[:, block],
+                    product[:, first : first + width],
+                    start=False,
+                    stop=e == P - 1 and column + width == BANK,
+                )
 
         stats = held.tile([P, HALVES * 6], F32, name="stats")
         for h in range(HALVES):

@@ -11,6 +11,7 @@ BANK = 512
 HALVES = N // BANK
 CHUNK = 16
 LAST_PIECE = 256
+X_PHASE = 128
 ALPHA = 0.25
 UNBIAS = ((N - 1) / N) ** 0.5
 
@@ -24,12 +25,13 @@ def tile_attention_kernel(tc, query, x, wx, wp, b1, offs, out):
         tc.tile_pool(name="held", bufs=1) as held,
         tc.tile_pool(name="windows", bufs=8) as windows,
         tc.tile_pool(name="products", bufs=3) as products,
+        tc.tile_pool(name="tokens", bufs=1) as tokens,
         tc.psum_pool(name="psum", bufs=1) as psum,
     ):
         offsets = lists.tile([P, N // 16], U16, name="offsets")
         nc.sync.dma_start(offsets[:], offs)
 
-        x_f32 = held.tile([P, N], F32, name="x_f32")
+        x_f32 = tokens.tile([P, N], F32, name="x_f32", offset=X_PHASE)
         nc.scalar.dma_start(x_f32[:], x)
         wx_tile = held.tile([P, P], BF16, name="wx_tile")
         nc.scalar.dma_start(wx_tile[:], wx)

@@ -10,7 +10,7 @@ N = 1024
 BANK = 512
 HALVES = N // BANK
 CHUNK = 16
-LAST_PIECE = 256
+PIECE = {P - 2: N // 2, P - 1: N // 4}
 X_PHASE = 128
 ALPHA = 0.25
 UNBIAS = ((N - 1) / N) ** 0.5
@@ -62,7 +62,7 @@ def tile_attention_kernel(tc, query, x, wx, wp, b1, offs, out):
                         u_psum[h][:], wx_tile[:], x_bf16[:, h * BANK : (h + 1) * BANK], start=True, stop=False
                     )
             product_f32 = products.tile([P, N], F32, name="product_f32")
-            piece = LAST_PIECE if e == P - 1 else N
+            piece = PIECE.get(e, N)
             for first in range(0, N, piece):
                 nc.vector.tensor_tensor(
                     product_f32[:, first : first + piece],

@@ -23,7 +23,7 @@ def tile_attention_kernel(tc, query, x, wx, wp, b1, offs, out):
     with (
         tc.tile_pool(name="lists", bufs=1) as lists,
         tc.tile_pool(name="held", bufs=1) as held,
-        tc.tile_pool(name="windows", bufs=8) as windows,
+        tc.tile_pool(name="windows", bufs=16) as windows,
         tc.tile_pool(name="products", bufs=3) as products,
         tc.tile_pool(name="tokens", bufs=1) as tokens,
         tc.psum_pool(name="psum", bufs=1) as psum,

import concourse.mybir as mybir

F32, BF16, U16 = mybir.dt.float32, mybir.dt.bfloat16, mybir.dt.uint16
MULT, ADD, POW = mybir.AluOpType.mult, mybir.AluOpType.add, mybir.AluOpType.pow
IDENTITY = mybir.ActivationFunctionType.Identity
SIGMOID = mybir.ActivationFunctionType.Sigmoid

P = 128
N = 1024
BANK = 512
HALVES = N // BANK
CHUNK = 16
PIECE = {P - 2: N // 2, P - 1: N // 4}
X_PHASE = 128
ALPHA = 0.25
UNBIAS = ((N - 1) / N) ** 0.5

FLOPS = 2 * (P * P + P) * P * N


def tile_attention_kernel(tc, query, x, wx, wp, b1, offs, out):
    nc = tc.nc
    with (
        tc.tile_pool(name="lists", bufs=1) as lists,
        tc.tile_pool(name="held", bufs=1) as held,
        tc.tile_pool(name="windows", bufs=16) as windows,
        tc.tile_pool(name="products", bufs=3) as products,
        tc.tile_pool(name="tokens", bufs=1) as tokens,
        tc.psum_pool(name="psum", bufs=1) as psum,
    ):
        offsets = lists.tile([P, N // 16], U16, name="offsets")
        nc.sync.dma_start(offsets[:], offs)

        x_f32 = tokens.tile([P, N], F32, name="x_f32", offset=X_PHASE)
        nc.scalar.dma_start(x_f32[:], x)
        wx_tile = held.tile([P, P], BF16, name="wx_tile")
        nc.scalar.dma_start(wx_tile[:], wx)
        bias = held.tile([P, 1], F32, name="bias")
        nc.scalar.dma_start(bias[:], b1)
        scaled_bias = held.tile([P, 1], F32, name="scaled_bias")
        nc.gpsimd.tensor_scalar(scaled_bias[:], bias[:], 1.0 - ALPHA, None, MULT)
        minus_half = held.tile([P, 1], F32, name="minus_half")
        nc.gpsimd.memset(minus_half[:], -0.5)
        warm = held.tile([P, 1], F32, name="warm")
        nc.scalar.activation(warm[:], minus_half[:], SIGMOID)

        wp_rows = wp.rearrange("(i e) m -> i (e m)", i=P)

        u_psum = [psum.tile([P, BANK], F32, name=f"u_psum{h}") for h in range(HALVES)]

        for e in range(P):
            window = windows.tile([P, N], F32, name="window")
            nc.sync.dma_start(window[:], query[e, :].partition_broadcast(P))
            if e % CHUNK == 0:
                wp_blocks = held.tile([P, CHUNK * P], BF16, name=f"wp_blocks{e // CHUNK}")
                nc.sync.dma_start(wp_blocks[:], wp_rows[:, e * P : (e + CHUNK) * P])
            if e == 0:
                x_bf16 = held.tile([P, N], BF16, name="x_bf16")
                nc.scalar.copy(x_bf16[:], x_f32[:])
                for h in range(HALVES):
                    nc.tensor.matmul(
                        u_psum[h][:], wx_tile[:], x_bf16[:, h * BANK : (h + 1) * BANK], start=True, stop=False
                    )
            product_f32 = products.tile([P, N], F32, name="product_f32")
            piece = PIECE.get(e, N)
            for first in range(0, N, piece):
                nc.vector.tensor_tensor(
                    product_f32[:, first : first + piece],
                    window[:].indirect(offsets[:, first // 16 : (first + piece) // 16]),
                    x_f32[:, first : first + piece],
                    MULT,
                )
            product = products.tile([P, N], BF16, name="product")
            for first in range(0, N, piece):
                if e == P - 1 and first + piece == N:
                    nc.vector.tensor_copy(product[:, first : first + piece], product_f32[:, first : first + piece])
                else:
                    nc.scalar.copy(product[:, first : first + piece], product_f32[:, first : first + piece])
            block = slice((e % CHUNK) * P, (e % CHUNK + 1) * P)
            width = min(piece, BANK)
            for first in range(0, N, width):
                h, column = first // BANK, first % BANK
                nc.tensor.matmul(
                    u_psum[h][:, column : column + width],
                    wp_blocks[:, block],
                    product[:, first : first + width],
                    start=False,
                    stop=e == P - 1 and column + width == BANK,
                )

        stats = held.tile([P, HALVES * 6], F32, name="stats")
        for h in range(HALVES):
            nc.vector.bn_stats(stats[:, h * 6 : (h + 1) * 6], u_psum[h][:])
        mean_var = held.tile([P, 2], F32, name="mean_var")
        nc.vector.bn_aggr(mean_var[:], stats[:])

        scaled_u = held.tile([P, N], F32, name="scaled_u")
        for h in range(HALVES):
            half = slice(h * BANK, (h + 1) * BANK)
            nc.scalar.activation(scaled_u[:, half], u_psum[h][:], IDENTITY, bias=scaled_bias[:, 0:1], scale=1.0 - ALPHA)

        inv_root = held.tile([P, 1], F32, name="inv_root")
        nc.gpsimd.tensor_tensor(inv_root[:], mean_var[:, 1:2], minus_half[:], POW)
        inv_std = held.tile([P, 1], F32, name="inv_std")
        nc.vector.tensor_scalar(inv_std[:], inv_root[:], UNBIAS, None, MULT)
        shift = held.tile([P, 1], F32, name="shift")
        nc.vector.tensor_scalar(shift[:], mean_var[:, 0:1], inv_root[:, 0:1], -UNBIAS, MULT, MULT)

        gate = held.tile([P, N], F32, name="gate")
        result = held.tile([P, N], F32, name="result")
        for h in range(HALVES):
            half = slice(h * BANK, (h + 1) * BANK)
            nc.scalar.activation(gate[:, half], u_psum[h][:], SIGMOID, bias=shift[:, 0:1], scale=inv_std[:, 0:1])
            nc.vector.scalar_tensor_tensor(
                result[:, half], gate[:, half], ALPHA / (1.0 - ALPHA), scaled_u[:, half], ADD, MULT
            )
            nc.sync.dma_start(out[:, half], result[:, half])
